import numpy as np
import ml_dtypes

BF16 = ml_dtypes.bfloat16


def bf(x):
    return np.asarray(x, np.float32).astype(BF16)


def f32(x):
    return np.asarray(x, np.float32)


def f64(x):
    return np.asarray(x).astype(np.float64)


def striped(idx):
    return np.tile(idx.reshape(-1, 16).T, (8, 1))


C, T, S, N = 256, 512, 1024, 128
TEMPERATURE = 0.1
TOKEN_SCALE = 3.0
BASE_SCALE = 0.2


def setup_inputs():
    return {"base": f32(BASE_SCALE * np.random.standard_normal((C, S))), "tokens": f32(TOKEN_SCALE * np.random.standard_normal((C, T))), "centroids": f32(np.random.standard_normal((C, N))), "offs": striped(np.random.permutation(S)[:N])}


def reference(base, tokens, centroids, offs):
    idx = offs[:16].T.reshape(-1)
    x = f64(tokens)
    cen = f64(centroids)
    nt = np.sqrt((x * x).sum(axis=0))
    nc = np.sqrt((cen * cen).sum(axis=0))
    sim = (x.T @ cen) / (nt[:, None] * nc[None, :] * TEMPERATURE)
    ex = np.exp(sim)
    a = ex / ex.sum(axis=1, keepdims=True)
    pooled = x @ a
    w = a.sum(axis=0)
    out = f64(base).copy()
    out[:, idx] = pooled * (1.0 / w)[None, :]
    return out

@@ -1,0 +1,109 @@
+import concourse.mybir as mybir
+from concourse.masks import make_identity
+
+P = 128
+C, T, S, N = 256, 512, 1024, 128
+CB = C // P
+TB = T // P
+TEMPERATURE = 0.1
+
+F32, BF16, U16 = mybir.dt.float32, mybir.dt.bfloat16, mybir.dt.uint16
+FUNC = mybir.ActivationFunctionType
+MULT = mybir.AluOpType.mult
+
+FLOPS = 2 * T * N * C + 2 * C * N * T
+
+
+def block(i):
+    return slice(i * P, (i + 1) * P)
+
+
+def tile_entityclusteringhead_kernel(tc, base, tokens, centroids, offs, out):
+    nc = tc.nc
+    with (
+        tc.tile_pool(name="held", bufs=1) as held,
+        tc.tile_pool(name="ring", bufs=2) as ring,
+        tc.psum_pool(name="flip_banks", bufs=2) as flip_banks,
+        tc.psum_pool(name="sim_banks", bufs=2) as sim_banks,
+        tc.psum_pool(name="sum_banks", bufs=1) as sum_banks,
+    ):
+        queue = [nc.sync, nc.scalar]
+        offsets = held.tile([P, N // 16], U16, name="offsets")
+        nc.sync.dma_start(offsets[:], offs)
+        cen = [held.tile([P, N], F32, name=f"cen{cb}") for cb in range(CB)]
+        tok = [held.tile([P, T], F32, name=f"tok{cb}") for cb in range(CB)]
+        window = [held.tile([P, S], F32, name=f"window{cb}") for cb in range(CB)]
+        for tiles, source in ((cen, centroids), (tok, tokens), (window, base)):
+            for cb in range(CB):
+                queue[cb].dma_start(tiles[cb][:], source[block(cb), :])
+
+        identity = held.tile([P, P], F32, name="identity")
+        make_identity(nc, identity[:])
+        ones = held.tile([P, P], BF16, name="ones")
+        nc.gpsimd.memset(ones[:], 1.0)
+
+        nc2 = sum_banks.tile([P, N], F32, name="nc2")
+        for cb in range(CB):
+            cen_sq = held.tile([P, N], BF16, name=f"cen_sq{cb}")
+            nc.gpsimd.tensor_tensor(cen_sq[:], cen[cb][:], cen[cb][:], MULT)
+            nc.tensor.matmul(nc2[:], ones[:], cen_sq[:], start=(cb == 0), stop=(cb == CB - 1))
+        norm_c = held.tile([P, N], F32, name="norm_c")
+        nc.scalar.activation(norm_c[:], nc2[:], FUNC.Sqrt)
+        inv_nc = held.tile([P, N], F32, name="inv_nc")
+        nc.vector.reciprocal(inv_nc[:], norm_c[:])
+        cen_unit = [held.tile([P, N], BF16, name=f"cen_unit{cb}") for cb in range(CB)]
+        for cb in range(CB):
+            nc.vector.tensor_tensor(cen_unit[cb][:], cen[cb][:], inv_nc[:], MULT)
+
+        tok_bf = [held.tile([P, T], BF16, name=f"tok_bf{cb}") for cb in range(CB)]
+        for cb in range(CB):
+            nc.vector.tensor_copy(tok_bf[cb][:], tok[cb][:])
+
+        nt2 = held.tile([P, TB], F32, name="nt2")
+        tokT_bf = [held.tile([P, C], BF16, name=f"tokT_bf{tb}") for tb in range(TB)]
+        for tb in range(TB):
+            flipped = flip_banks.tile([P, C], F32, name="flipped")
+            for cb in range(CB):
+                nc.tensor.transpose(flipped[:, block(cb)], tok[cb][:, block(tb)], identity[:])
+            squares = ring.tile([P, C], BF16, name="squares")
+            nc.scalar.activation(
+                squares[:], flipped[:], FUNC.Square, scale=TEMPERATURE, accum_out=nt2[:, tb : tb + 1]
+            )
+            nc.vector.tensor_copy(tokT_bf[tb][:], flipped[:])
+        norm_t = held.tile([P, TB], F32, name="norm_t")
+        nc.scalar.activation(norm_t[:], nt2[:], FUNC.Sqrt)
+        sharp = held.tile([P, TB], F32, name="sharp")
+        nc.vector.reciprocal(sharp[:], norm_t[:])
+
+        exp_sum = held.tile([P, TB], F32, name="exp_sum")
+        inv_exp_sum = held.tile([P, TB], F32, name="inv_exp_sum")
+        w = sum_banks.tile([P, N], F32, name="w")
+        pooled = [sum_banks.tile([P, N], F32, name=f"pooled{cb}") for cb in range(CB)]
+        for tb in range(TB):
+            sim = sim_banks.tile([P, N], F32, name="sim")
+            for cb in range(CB):
+                nc.tensor.matmul(
+                    sim[:], tok_bf[cb][:, block(tb)], cen_unit[cb][:], start=(cb == 0), stop=(cb == CB - 1)
+                )
+            exp_sim = ring.tile([P, N], F32, name="exp_sim")
+            nc.scalar.activation(
+                exp_sim[:], sim[:], FUNC.Exp, scale=sharp[:, tb : tb + 1], accum_out=exp_sum[:, tb : tb + 1]
+            )
+            nc.vector.reciprocal(inv_exp_sum[:, tb : tb + 1], exp_sum[:, tb : tb + 1])
+            a = ring.tile([P, N], BF16, name="a")
+            nc.vector.tensor_scalar_mul(a[:], exp_sim[:], inv_exp_sum[:, tb : tb + 1])
+            nc.tensor.matmul(w[:], ones[:], a[:], start=(tb == 0), stop=(tb == TB - 1))
+            for cb in range(CB):
+                nc.tensor.matmul(
+                    pooled[cb][:], tokT_bf[tb][:, block(cb)], a[:], start=(tb == 0), stop=(tb == TB - 1)
+                )
+
+        inv_w = held.tile([P, N], F32, name="inv_w")
+        nc.vector.reciprocal(inv_w[:], w[:])
+        pooled_sb = [held.tile([P, N], F32, name=f"pooled_sb{cb}") for cb in range(CB)]
+        for cb in range(CB):
+            nc.scalar.copy(pooled_sb[cb][:], pooled[cb][:])
+
+        for cb in range(CB):
+            nc.vector.tensor_tensor(window[cb][:].indirect(offsets[:]), pooled_sb[cb][:], inv_w[:], MULT)
+            queue[cb].dma_start(out[block(cb), :], window[cb][:])

@@ -9,7 +9,7 @@ TEMPERATURE = 0.1
 
 F32, BF16, U16 = mybir.dt.float32, mybir.dt.bfloat16, mybir.dt.uint16
 FUNC = mybir.ActivationFunctionType
-MULT = mybir.AluOpType.mult
+MULT, POW = mybir.AluOpType.mult, mybir.AluOpType.pow
 
 FLOPS = 2 * T * N * C + 2 * C * N * T
 
@@ -23,9 +23,7 @@ def tile_entityclusteringhead_kernel(tc, base, tokens, centroids, offs, out):
     with (
         tc.tile_pool(name="held", bufs=1) as held,
         tc.tile_pool(name="ring", bufs=2) as ring,
-        tc.psum_pool(name="flip_banks", bufs=2) as flip_banks,
         tc.psum_pool(name="sim_banks", bufs=2) as sim_banks,
-        tc.psum_pool(name="sum_banks", bufs=1) as sum_banks,
     ):
         queue = [nc.sync, nc.scalar]
         offsets = held.tile([P, N // 16], U16, name="offsets")
@@ -41,68 +39,75 @@ def tile_entityclusteringhead_kernel(tc, base, tokens, centroids, offs, out):
         make_identity(nc, identity[:])
         ones = held.tile([P, P], BF16, name="ones")
         nc.gpsimd.memset(ones[:], 1.0)
+        minus_half = held.tile([P, 1], F32, name="minus_half")
+        nc.gpsimd.memset(minus_half[:], -0.5)
 
-        nc2 = sum_banks.tile([P, N], F32, name="nc2")
-        for cb in range(CB):
-            cen_sq = held.tile([P, N], BF16, name=f"cen_sq{cb}")
-            nc.gpsimd.tensor_tensor(cen_sq[:], cen[cb][:], cen[cb][:], MULT)
-            nc.tensor.matmul(nc2[:], ones[:], cen_sq[:], start=(cb == 0), stop=(cb == CB - 1))
-        norm_c = held.tile([P, N], F32, name="norm_c")
-        nc.scalar.activation(norm_c[:], nc2[:], FUNC.Sqrt)
-        inv_nc = held.tile([P, N], F32, name="inv_nc")
-        nc.vector.reciprocal(inv_nc[:], norm_c[:])
         cen_unit = [held.tile([P, N], BF16, name=f"cen_unit{cb}") for cb in range(CB)]
-        for cb in range(CB):
-            nc.vector.tensor_tensor(cen_unit[cb][:], cen[cb][:], inv_nc[:], MULT)
-
         tok_bf = [held.tile([P, T], BF16, name=f"tok_bf{cb}") for cb in range(CB)]
-        for cb in range(CB):
-            nc.vector.tensor_copy(tok_bf[cb][:], tok[cb][:])
-
-        nt2 = held.tile([P, TB], F32, name="nt2")
         tokT_bf = [held.tile([P, C], BF16, name=f"tokT_bf{tb}") for tb in range(TB)]
-        for tb in range(TB):
-            flipped = flip_banks.tile([P, C], F32, name="flipped")
-            for cb in range(CB):
-                nc.tensor.transpose(flipped[:, block(cb)], tok[cb][:, block(tb)], identity[:])
-            squares = ring.tile([P, C], BF16, name="squares")
-            nc.scalar.activation(
-                squares[:], flipped[:], FUNC.Square, scale=TEMPERATURE, accum_out=nt2[:, tb : tb + 1]
-            )
-            nc.vector.tensor_copy(tokT_bf[tb][:], flipped[:])
-        norm_t = held.tile([P, TB], F32, name="norm_t")
-        nc.scalar.activation(norm_t[:], nt2[:], FUNC.Sqrt)
+        nt2 = held.tile([P, TB], F32, name="nt2")
         sharp = held.tile([P, TB], F32, name="sharp")
-        nc.vector.reciprocal(sharp[:], norm_t[:])
-
-        exp_sum = held.tile([P, TB], F32, name="exp_sum")
-        inv_exp_sum = held.tile([P, TB], F32, name="inv_exp_sum")
-        w = sum_banks.tile([P, N], F32, name="w")
-        pooled = [sum_banks.tile([P, N], F32, name=f"pooled{cb}") for cb in range(CB)]
-        for tb in range(TB):
-            sim = sim_banks.tile([P, N], F32, name="sim")
+        with (
+            tc.psum_pool(name="cen_banks", bufs=1) as cen_banks,
+            tc.psum_pool(name="flip_banks", bufs=TB) as flip_banks,
+        ):
+            nc2 = cen_banks.tile([P, 1], F32, name="nc2")
             for cb in range(CB):
-                nc.tensor.matmul(
-                    sim[:], tok_bf[cb][:, block(tb)], cen_unit[cb][:], start=(cb == 0), stop=(cb == CB - 1)
-                )
-            exp_sim = ring.tile([P, N], F32, name="exp_sim")
-            nc.scalar.activation(
-                exp_sim[:], sim[:], FUNC.Exp, scale=sharp[:, tb : tb + 1], accum_out=exp_sum[:, tb : tb + 1]
-            )
-            nc.vector.reciprocal(inv_exp_sum[:, tb : tb + 1], exp_sum[:, tb : tb + 1])
-            a = ring.tile([P, N], BF16, name="a")
-            nc.vector.tensor_scalar_mul(a[:], exp_sim[:], inv_exp_sum[:, tb : tb + 1])
-            nc.tensor.matmul(w[:], ones[:], a[:], start=(tb == 0), stop=(tb == TB - 1))
-            for cb in range(CB):
-                nc.tensor.matmul(
-                    pooled[cb][:], tokT_bf[tb][:, block(cb)], a[:], start=(tb == 0), stop=(tb == TB - 1)
-                )
+                cen_sq = held.tile([P, N], BF16, name=f"cen_sq{cb}")
+                nc.vector.tensor_tensor(cen_sq[:], cen[cb][:], cen[cb][:], MULT)
+                nc.tensor.matmul(nc2[:], cen_sq[:], ones[:, 0:1], start=(cb == 0), stop=(cb == CB - 1))
+            nc2_sb = held.tile([P, 1], F32, name="nc2_sb")
+            nc.vector.tensor_copy(nc2_sb[:], nc2[:])
+            inv_nc = held.tile([P, 1], F32, name="inv_nc")
+            nc.gpsimd.tensor_tensor(inv_nc[:], nc2_sb[:], minus_half[:], POW)
 
-        inv_w = held.tile([P, N], F32, name="inv_w")
-        nc.vector.reciprocal(inv_w[:], w[:])
-        pooled_sb = [held.tile([P, N], F32, name=f"pooled_sb{cb}") for cb in range(CB)]
-        for cb in range(CB):
-            nc.scalar.copy(pooled_sb[cb][:], pooled[cb][:])
+            for cb in range(CB):
+                nc.vector.tensor_copy(tok_bf[cb][:], tok[cb][:])
+            for tb in range(TB):
+                flipped = flip_banks.tile([P, C], F32, name="flipped")
+                for cb in range(CB):
+                    nc.tensor.transpose(flipped[:, block(cb)], tok[cb][:, block(tb)], identity[:])
+                squares = ring.tile([P, C], BF16, name="squares")
+                nc.scalar.activation(
+                    squares[:], flipped[:], FUNC.Square, scale=TEMPERATURE, accum_out=nt2[:, tb : tb + 1]
+                )
+                nc.gpsimd.tensor_tensor(sharp[:, tb : tb + 1], nt2[:, tb : tb + 1], minus_half[:], POW)
+                nc.vector.tensor_copy(tokT_bf[tb][:], flipped[:])
+
+            spread = cen_banks.tile([P, N], F32, name="spread")
+            nc.tensor.matmul(spread[:], inv_nc[:, 0:1].to_broadcast([P, P]), identity[:], start=True, stop=True)
+            for cb in range(CB):
+                nc.vector.tensor_tensor(cen_unit[cb][:], cen[cb][:], spread[:], MULT)
+
+        with tc.psum_pool(name="sum_banks", bufs=1) as sum_banks:
+            exp_sum = held.tile([P, TB], F32, name="exp_sum")
+            inv_exp_sum = held.tile([P, TB], F32, name="inv_exp_sum")
+            w = sum_banks.tile([P, N], F32, name="w")
+            pooled = [sum_banks.tile([P, N], F32, name=f"pooled{cb}") for cb in range(CB)]
+            for tb in range(TB):
+                sim = sim_banks.tile([P, N], F32, name="sim")
+                for cb in range(CB):
+                    nc.tensor.matmul(
+                        sim[:], tok_bf[cb][:, block(tb)], cen_unit[cb][:], start=(cb == 0), stop=(cb == CB - 1)
+                    )
+                exp_sim = ring.tile([P, N], F32, name="exp_sim")
+                nc.scalar.activation(
+                    exp_sim[:], sim[:], FUNC.Exp, scale=sharp[:, tb : tb + 1], accum_out=exp_sum[:, tb : tb + 1]
+                )
+                nc.vector.reciprocal(inv_exp_sum[:, tb : tb + 1], exp_sum[:, tb : tb + 1])
+                a = ring.tile([P, N], BF16, name="a")
+                nc.vector.tensor_scalar_mul(a[:], exp_sim[:], inv_exp_sum[:, tb : tb + 1])
+                nc.tensor.matmul(w[:], ones[:], a[:], start=(tb == 0), stop=(tb == TB - 1))
+                for cb in range(CB):
+                    nc.tensor.matmul(
+                        pooled[cb][:], tokT_bf[tb][:, block(cb)], a[:], start=(tb == 0), stop=(tb == TB - 1)
+                    )
+
+            inv_w = held.tile([P, N], F32, name="inv_w")
+            nc.vector.reciprocal(inv_w[:], w[:])
+            pooled_sb = [held.tile([P, N], F32, name=f"pooled_sb{cb}") for cb in range(CB)]
+            for cb in range(CB):
+                nc.scalar.copy(pooled_sb[cb][:], pooled[cb][:])
 
         for cb in range(CB):
             nc.vector.tensor_tensor(window[cb][:].indirect(offsets[:]), pooled_sb[cb][:], inv_w[:], MULT)

@@ -5,7 +5,11 @@ P = 128
 C, T, S, N = 256, 512, 1024, 128
 CB = C // P
 TB = T // P
+TG = 2
+GB = TB // TG
 TEMPERATURE = 0.1
+BANK = 512
+WARM_UP = 3
 
 F32, BF16, U16 = mybir.dt.float32, mybir.dt.bfloat16, mybir.dt.uint16
 FUNC = mybir.ActivationFunctionType
@@ -26,24 +30,35 @@ def tile_entityclusteringhead_kernel(tc, base, tokens, centroids, offs, out):
         tc.psum_pool(name="sim_banks", bufs=2) as sim_banks,
     ):
         queue = [nc.sync, nc.scalar]
-        offsets = held.tile([P, N // 16], U16, name="offsets")
-        nc.sync.dma_start(offsets[:], offs)
         cen = [held.tile([P, N], F32, name=f"cen{cb}") for cb in range(CB)]
-        tok = [held.tile([P, T], F32, name=f"tok{cb}") for cb in range(CB)]
+        tok = [[held.tile([P, GB * P], F32, name=f"tok{cb}_{g}") for g in range(TG)] for cb in range(CB)]
+        offsets = held.tile([P, N // 16], U16, name="offsets")
         window = [held.tile([P, S], F32, name=f"window{cb}") for cb in range(CB)]
-        for tiles, source in ((cen, centroids), (tok, tokens), (window, base)):
+        for cb in range(CB):
+            queue[cb].dma_start(cen[cb][:], centroids[block(cb), :])
+        for g in range(TG):
             for cb in range(CB):
-                queue[cb].dma_start(tiles[cb][:], source[block(cb), :])
+                queue[cb].dma_start(tok[cb][g][:], tokens[block(cb), g * GB * P : (g + 1) * GB * P])
+        nc.sync.dma_start(offsets[:], offs)
+        for cb in range(CB):
+            queue[cb].dma_start(window[cb][:], base[block(cb), :])
 
-        identity = held.tile([P, P], F32, name="identity")
-        make_identity(nc, identity[:])
+        zeros = held.tile([P, BANK], BF16, name="zeros")
+        nc.vector.memset(zeros[:], 0.0)
         ones = held.tile([P, P], BF16, name="ones")
         nc.gpsimd.memset(ones[:], 1.0)
+        identity = held.tile([P, P], F32, name="identity")
+        make_identity(nc, identity[:])
         minus_half = held.tile([P, 1], F32, name="minus_half")
         nc.gpsimd.memset(minus_half[:], -0.5)
 
+        with tc.psum_pool(name="warm_bank", bufs=1) as warm_bank:
+            warm = warm_bank.tile([P, BANK], F32, name="warm")
+            for i in range(WARM_UP):
+                nc.tensor.matmul(warm[:], zeros[:, 0:P], zeros[:], start=True, stop=True)
+
         cen_unit = [held.tile([P, N], BF16, name=f"cen_unit{cb}") for cb in range(CB)]
-        tok_bf = [held.tile([P, T], BF16, name=f"tok_bf{cb}") for cb in range(CB)]
+        tok_bf = [[held.tile([P, GB * P], BF16, name=f"tok_bf{cb}_{g}") for g in range(TG)] for cb in range(CB)]
         tokT_bf = [held.tile([P, C], BF16, name=f"tokT_bf{tb}") for tb in range(TB)]
         nt2 = held.tile([P, TB], F32, name="nt2")
         sharp = held.tile([P, TB], F32, name="sharp")
@@ -51,6 +66,22 @@ def tile_entityclusteringhead_kernel(tc, base, tokens, centroids, offs, out):
             tc.psum_pool(name="cen_banks", bufs=1) as cen_banks,
             tc.psum_pool(name="flip_banks", bufs=TB) as flip_banks,
         ):
+
+            def prepare_tokens(g):
+                for cb in range(CB):
+                    nc.vector.tensor_copy(tok_bf[cb][g][:], tok[cb][g][:])
+                for b in range(GB):
+                    tb = g * GB + b
+                    flipped = flip_banks.tile([P, C], F32, name="flipped")
+                    for cb in range(CB):
+                        nc.tensor.transpose(flipped[:, block(cb)], tok[cb][g][:, block(b)], identity[:])
+                    squares = ring.tile([P, C], BF16, name="squares")
+                    nc.scalar.activation(
+                        squares[:], flipped[:], FUNC.Square, scale=TEMPERATURE, accum_out=nt2[:, tb : tb + 1]
+                    )
+                    nc.gpsimd.tensor_tensor(sharp[:, tb : tb + 1], nt2[:, tb : tb + 1], minus_half[:], POW)
+                    nc.vector.tensor_copy(tokT_bf[tb][:], flipped[:])
+
             nc2 = cen_banks.tile([P, 1], F32, name="nc2")
             for cb in range(CB):
                 cen_sq = held.tile([P, N], BF16, name=f"cen_sq{cb}")
@@ -61,23 +92,14 @@ def tile_entityclusteringhead_kernel(tc, base, tokens, centroids, offs, out):
             inv_nc = held.tile([P, 1], F32, name="inv_nc")
             nc.gpsimd.tensor_tensor(inv_nc[:], nc2_sb[:], minus_half[:], POW)
 
-            for cb in range(CB):
-                nc.vector.tensor_copy(tok_bf[cb][:], tok[cb][:])
-            for tb in range(TB):
-                flipped = flip_banks.tile([P, C], F32, name="flipped")
-                for cb in range(CB):
-                    nc.tensor.transpose(flipped[:, block(cb)], tok[cb][:, block(tb)], identity[:])
-                squares = ring.tile([P, C], BF16, name="squares")
-                nc.scalar.activation(
-                    squares[:], flipped[:], FUNC.Square, scale=TEMPERATURE, accum_out=nt2[:, tb : tb + 1]
-                )
-                nc.gpsimd.tensor_tensor(sharp[:, tb : tb + 1], nt2[:, tb : tb + 1], minus_half[:], POW)
-                nc.vector.tensor_copy(tokT_bf[tb][:], flipped[:])
+            prepare_tokens(0)
 
             spread = cen_banks.tile([P, N], F32, name="spread")
             nc.tensor.matmul(spread[:], inv_nc[:, 0:1].to_broadcast([P, P]), identity[:], start=True, stop=True)
             for cb in range(CB):
                 nc.vector.tensor_tensor(cen_unit[cb][:], cen[cb][:], spread[:], MULT)
+
+            prepare_tokens(1)
 
         with tc.psum_pool(name="sum_banks", bufs=1) as sum_banks:
             exp_sum = held.tile([P, TB], F32, name="exp_sum")
@@ -88,7 +110,11 @@ def tile_entityclusteringhead_kernel(tc, base, tokens, centroids, offs, out):
                 sim = sim_banks.tile([P, N], F32, name="sim")
                 for cb in range(CB):
                     nc.tensor.matmul(
-                        sim[:], tok_bf[cb][:, block(tb)], cen_unit[cb][:], start=(cb == 0), stop=(cb == CB - 1)
+                        sim[:],
+                        tok_bf[cb][tb // GB][:, block(tb % GB)],
+                        cen_unit[cb][:],
+                        start=(cb == 0),
+                        stop=(cb == CB - 1),
                     )
                 exp_sim = ring.tile([P, N], F32, name="exp_sim")
                 nc.scalar.activation(

@@ -29,19 +29,17 @@ def tile_entityclusteringhead_kernel(tc, base, tokens, centroids, offs, out):
         tc.tile_pool(name="ring", bufs=2) as ring,
         tc.psum_pool(name="sim_banks", bufs=2) as sim_banks,
     ):
-        queue = [nc.sync, nc.scalar]
-        cen = [held.tile([P, N], F32, name=f"cen{cb}") for cb in range(CB)]
-        tok = [[held.tile([P, GB * P], F32, name=f"tok{cb}_{g}") for g in range(TG)] for cb in range(CB)]
+        cen = held.tile([P, CB, N], F32, name="cen")
+        tok = [held.tile([P, CB, GB * P], F32, name=f"tok{g}") for g in range(TG)]
         offsets = held.tile([P, N // 16], U16, name="offsets")
         window = [held.tile([P, S], F32, name=f"window{cb}") for cb in range(CB)]
-        for cb in range(CB):
-            queue[cb].dma_start(cen[cb][:], centroids[block(cb), :])
-        for g in range(TG):
-            for cb in range(CB):
-                queue[cb].dma_start(tok[cb][g][:], tokens[block(cb), g * GB * P : (g + 1) * GB * P])
+        tokens_by_block = tokens.rearrange("(cb p) t -> p cb t", p=P)
+        nc.sync.dma_start(cen[:], centroids.rearrange("(cb p) j -> p cb j", p=P))
+        nc.scalar.dma_start(tok[0][:], tokens_by_block[:, :, 0 : GB * P])
+        nc.sync.dma_start(tok[1][:], tokens_by_block[:, :, GB * P : T])
         nc.sync.dma_start(offsets[:], offs)
-        for cb in range(CB):
-            queue[cb].dma_start(window[cb][:], base[block(cb), :])
+        nc.scalar.dma_start(window[0][:], base[block(0), :])
+        nc.sync.dma_start(window[1][:], base[block(1), :])
 
         zeros = held.tile([P, BANK], BF16, name="zeros")
         nc.vector.memset(zeros[:], 0.0)
@@ -49,7 +47,7 @@ def tile_entityclusteringhead_kernel(tc, base, tokens, centroids, offs, out):
         nc.gpsimd.memset(ones[:], 1.0)
         identity = held.tile([P, P], F32, name="identity")
         make_identity(nc, identity[:])
-        minus_half = held.tile([P, 1], F32, name="minus_half")
+        minus_half = held.tile([P, GB], F32, name="minus_half")
         nc.gpsimd.memset(minus_half[:], -0.5)
 
         with tc.psum_pool(name="warm_bank", bufs=1) as warm_bank:
@@ -57,8 +55,8 @@ def tile_entityclusteringhead_kernel(tc, base, tokens, centroids, offs, out):
             for i in range(WARM_UP):
                 nc.tensor.matmul(warm[:], zeros[:, 0:P], zeros[:], start=True, stop=True)
 
-        cen_unit = [held.tile([P, N], BF16, name=f"cen_unit{cb}") for cb in range(CB)]
-        tok_bf = [[held.tile([P, GB * P], BF16, name=f"tok_bf{cb}_{g}") for g in range(TG)] for cb in range(CB)]
+        cen_unit = held.tile([P, CB, N], BF16, name="cen_unit")
+        tok_bf = [held.tile([P, CB, GB * P], BF16, name=f"tok_bf{g}") for g in range(TG)]
         tokT_bf = [held.tile([P, C], BF16, name=f"tokT_bf{tb}") for tb in range(TB)]
         nt2 = held.tile([P, TB], F32, name="nt2")
         sharp = held.tile([P, TB], F32, name="sharp")
@@ -68,36 +66,35 @@ def tile_entityclusteringhead_kernel(tc, base, tokens, centroids, offs, out):
         ):
 
             def prepare_tokens(g):
-                for cb in range(CB):
-                    nc.vector.tensor_copy(tok_bf[cb][g][:], tok[cb][g][:])
+                nc.vector.tensor_copy(tok_bf[g][:], tok[g][:])
                 for b in range(GB):
                     tb = g * GB + b
                     flipped = flip_banks.tile([P, C], F32, name="flipped")
                     for cb in range(CB):
-                        nc.tensor.transpose(flipped[:, block(cb)], tok[cb][g][:, block(b)], identity[:])
+                        nc.tensor.transpose(flipped[:, block(cb)], tok[g][:, cb, block(b)], identity[:])
                     squares = ring.tile([P, C], BF16, name="squares")
                     nc.scalar.activation(
                         squares[:], flipped[:], FUNC.Square, scale=TEMPERATURE, accum_out=nt2[:, tb : tb + 1]
                     )
-                    nc.gpsimd.tensor_tensor(sharp[:, tb : tb + 1], nt2[:, tb : tb + 1], minus_half[:], POW)
                     nc.vector.tensor_copy(tokT_bf[tb][:], flipped[:])
+                group = slice(g * GB, (g + 1) * GB)
+                nc.gpsimd.tensor_tensor(sharp[:, group], nt2[:, group], minus_half[:], POW)
 
+            cen_sq = held.tile([P, CB, N], BF16, name="cen_sq")
+            nc.vector.tensor_tensor(cen_sq[:], cen[:], cen[:], MULT)
             nc2 = cen_banks.tile([P, 1], F32, name="nc2")
             for cb in range(CB):
-                cen_sq = held.tile([P, N], BF16, name=f"cen_sq{cb}")
-                nc.vector.tensor_tensor(cen_sq[:], cen[cb][:], cen[cb][:], MULT)
-                nc.tensor.matmul(nc2[:], cen_sq[:], ones[:, 0:1], start=(cb == 0), stop=(cb == CB - 1))
+                nc.tensor.matmul(nc2[:], cen_sq[:, cb, :], ones[:, 0:1], start=(cb == 0), stop=(cb == CB - 1))
             nc2_sb = held.tile([P, 1], F32, name="nc2_sb")
             nc.vector.tensor_copy(nc2_sb[:], nc2[:])
             inv_nc = held.tile([P, 1], F32, name="inv_nc")
-            nc.gpsimd.tensor_tensor(inv_nc[:], nc2_sb[:], minus_half[:], POW)
+            nc.gpsimd.tensor_tensor(inv_nc[:], nc2_sb[:], minus_half[:, 0:1], POW)
 
             prepare_tokens(0)
 
             spread = cen_banks.tile([P, N], F32, name="spread")
             nc.tensor.matmul(spread[:], inv_nc[:, 0:1].to_broadcast([P, P]), identity[:], start=True, stop=True)
-            for cb in range(CB):
-                nc.vector.tensor_tensor(cen_unit[cb][:], cen[cb][:], spread[:], MULT)
+            nc.vector.tensor_tensor(cen_unit[:], cen[:], spread[:].unsqueeze(1).to_broadcast([P, CB, N]), MULT)
 
             prepare_tokens(1)
 
@@ -111,8 +108,8 @@ def tile_entityclusteringhead_kernel(tc, base, tokens, centroids, offs, out):
                 for cb in range(CB):
                     nc.tensor.matmul(
                         sim[:],
-                        tok_bf[cb][tb // GB][:, block(tb % GB)],
-                        cen_unit[cb][:],
+                        tok_bf[tb // GB][:, cb, block(tb % GB)],
+                        cen_unit[:, cb, :],
                         start=(cb == 0),
                         stop=(cb == CB - 1),
                     )
@@ -135,6 +132,7 @@ def tile_entityclusteringhead_kernel(tc, base, tokens, centroids, offs, out):
             for cb in range(CB):
                 nc.scalar.copy(pooled_sb[cb][:], pooled[cb][:])
 
+        store_queue = [nc.sync, nc.scalar]
         for cb in range(CB):
             nc.vector.tensor_tensor(window[cb][:].indirect(offsets[:]), pooled_sb[cb][:], inv_w[:], MULT)
-            queue[cb].dma_start(out[block(cb), :], window[cb][:])
+            store_queue[cb].dma_start(out[block(cb), :], window[cb][:])

@@ -7,6 +7,7 @@ CB = C // P
 TB = T // P
 TG = 2
 GB = TB // TG
+STORE_PIECES = 4
 TEMPERATURE = 0.1
 BANK = 512
 WARM_UP = 3
@@ -29,17 +30,19 @@ def tile_entityclusteringhead_kernel(tc, base, tokens, centroids, offs, out):
         tc.tile_pool(name="ring", bufs=2) as ring,
         tc.psum_pool(name="sim_banks", bufs=2) as sim_banks,
     ):
-        cen = held.tile([P, CB, N], F32, name="cen")
-        tok = [held.tile([P, CB, GB * P], F32, name=f"tok{g}") for g in range(TG)]
+        queue = [nc.sync, nc.scalar]
+        cen = [held.tile([P, N], F32, name=f"cen{cb}") for cb in range(CB)]
+        tok = [[held.tile([P, GB * P], F32, name=f"tok{cb}_{g}") for g in range(TG)] for cb in range(CB)]
         offsets = held.tile([P, N // 16], U16, name="offsets")
         window = [held.tile([P, S], F32, name=f"window{cb}") for cb in range(CB)]
-        tokens_by_block = tokens.rearrange("(cb p) t -> p cb t", p=P)
-        nc.sync.dma_start(cen[:], centroids.rearrange("(cb p) j -> p cb j", p=P))
-        nc.scalar.dma_start(tok[0][:], tokens_by_block[:, :, 0 : GB * P])
-        nc.sync.dma_start(tok[1][:], tokens_by_block[:, :, GB * P : T])
+        for cb in range(CB):
+            queue[cb].dma_start(cen[cb][:], centroids[block(cb), :])
+        for g in range(TG):
+            for cb in range(CB):
+                queue[cb].dma_start(tok[cb][g][:], tokens[block(cb), g * GB * P : (g + 1) * GB * P])
         nc.sync.dma_start(offsets[:], offs)
-        nc.scalar.dma_start(window[0][:], base[block(0), :])
-        nc.sync.dma_start(window[1][:], base[block(1), :])
+        for cb in range(CB):
+            queue[cb].dma_start(window[cb][:], base[block(cb), :])
 
         zeros = held.tile([P, BANK], BF16, name="zeros")
         nc.vector.memset(zeros[:], 0.0)
@@ -47,7 +50,7 @@ def tile_entityclusteringhead_kernel(tc, base, tokens, centroids, offs, out):
         nc.gpsimd.memset(ones[:], 1.0)
         identity = held.tile([P, P], F32, name="identity")
         make_identity(nc, identity[:])
-        minus_half = held.tile([P, GB], F32, name="minus_half")
+        minus_half = held.tile([P, 1], F32, name="minus_half")
         nc.gpsimd.memset(minus_half[:], -0.5)
 
         with tc.psum_pool(name="warm_bank", bufs=1) as warm_bank:
@@ -55,8 +58,8 @@ def tile_entityclusteringhead_kernel(tc, base, tokens, centroids, offs, out):
             for i in range(WARM_UP):
                 nc.tensor.matmul(warm[:], zeros[:, 0:P], zeros[:], start=True, stop=True)
 
-        cen_unit = held.tile([P, CB, N], BF16, name="cen_unit")
-        tok_bf = [held.tile([P, CB, GB * P], BF16, name=f"tok_bf{g}") for g in range(TG)]
+        cen_unit = [held.tile([P, N], BF16, name=f"cen_unit{cb}") for cb in range(CB)]
+        tok_bf = [[held.tile([P, GB * P], BF16, name=f"tok_bf{cb}_{g}") for g in range(TG)] for cb in range(CB)]
         tokT_bf = [held.tile([P, C], BF16, name=f"tokT_bf{tb}") for tb in range(TB)]
         nt2 = held.tile([P, TB], F32, name="nt2")
         sharp = held.tile([P, TB], F32, name="sharp")
@@ -66,35 +69,36 @@ def tile_entityclusteringhead_kernel(tc, base, tokens, centroids, offs, out):
         ):
 
             def prepare_tokens(g):
-                nc.vector.tensor_copy(tok_bf[g][:], tok[g][:])
+                for cb in range(CB):
+                    nc.vector.tensor_copy(tok_bf[cb][g][:], tok[cb][g][:])
                 for b in range(GB):
                     tb = g * GB + b
                     flipped = flip_banks.tile([P, C], F32, name="flipped")
                     for cb in range(CB):
-                        nc.tensor.transpose(flipped[:, block(cb)], tok[g][:, cb, block(b)], identity[:])
+                        nc.tensor.transpose(flipped[:, block(cb)], tok[cb][g][:, block(b)], identity[:])
                     squares = ring.tile([P, C], BF16, name="squares")
                     nc.scalar.activation(
                         squares[:], flipped[:], FUNC.Square, scale=TEMPERATURE, accum_out=nt2[:, tb : tb + 1]
                     )
+                    nc.gpsimd.tensor_tensor(sharp[:, tb : tb + 1], nt2[:, tb : tb + 1], minus_half[:], POW)
                     nc.vector.tensor_copy(tokT_bf[tb][:], flipped[:])
-                group = slice(g * GB, (g + 1) * GB)
-                nc.gpsimd.tensor_tensor(sharp[:, group], nt2[:, group], minus_half[:], POW)
 
-            cen_sq = held.tile([P, CB, N], BF16, name="cen_sq")
-            nc.vector.tensor_tensor(cen_sq[:], cen[:], cen[:], MULT)
             nc2 = cen_banks.tile([P, 1], F32, name="nc2")
             for cb in range(CB):
-                nc.tensor.matmul(nc2[:], cen_sq[:, cb, :], ones[:, 0:1], start=(cb == 0), stop=(cb == CB - 1))
+                cen_sq = held.tile([P, N], BF16, name=f"cen_sq{cb}")
+                nc.vector.tensor_tensor(cen_sq[:], cen[cb][:], cen[cb][:], MULT)
+                nc.tensor.matmul(nc2[:], cen_sq[:], ones[:, 0:1], start=(cb == 0), stop=(cb == CB - 1))
             nc2_sb = held.tile([P, 1], F32, name="nc2_sb")
             nc.vector.tensor_copy(nc2_sb[:], nc2[:])
             inv_nc = held.tile([P, 1], F32, name="inv_nc")
-            nc.gpsimd.tensor_tensor(inv_nc[:], nc2_sb[:], minus_half[:, 0:1], POW)
+            nc.gpsimd.tensor_tensor(inv_nc[:], nc2_sb[:], minus_half[:], POW)
 
             prepare_tokens(0)
 
             spread = cen_banks.tile([P, N], F32, name="spread")
             nc.tensor.matmul(spread[:], inv_nc[:, 0:1].to_broadcast([P, P]), identity[:], start=True, stop=True)
-            nc.vector.tensor_tensor(cen_unit[:], cen[:], spread[:].unsqueeze(1).to_broadcast([P, CB, N]), MULT)
+            for cb in range(CB):
+                nc.vector.tensor_tensor(cen_unit[cb][:], cen[cb][:], spread[:], MULT)
 
             prepare_tokens(1)
 
@@ -108,8 +112,8 @@ def tile_entityclusteringhead_kernel(tc, base, tokens, centroids, offs, out):
                 for cb in range(CB):
                     nc.tensor.matmul(
                         sim[:],
-                        tok_bf[tb // GB][:, cb, block(tb % GB)],
-                        cen_unit[:, cb, :],
+                        tok_bf[cb][tb // GB][:, block(tb % GB)],
+                        cen_unit[cb][:],
                         start=(cb == 0),
                         stop=(cb == CB - 1),
                     )
@@ -132,7 +136,8 @@ def tile_entityclusteringhead_kernel(tc, base, tokens, centroids, offs, out):
             for cb in range(CB):
                 nc.scalar.copy(pooled_sb[cb][:], pooled[cb][:])
 
-        store_queue = [nc.sync, nc.scalar]
         for cb in range(CB):
             nc.vector.tensor_tensor(window[cb][:].indirect(offsets[:]), pooled_sb[cb][:], inv_w[:], MULT)
-            store_queue[cb].dma_start(out[block(cb), :], window[cb][:])
+            for piece in range(STORE_PIECES):
+                columns = slice(piece * S // STORE_PIECES, (piece + 1) * S // STORE_PIECES)
+                queue[piece % 2].dma_start(out[block(cb), columns], window[cb][:, columns])

@@ -7,10 +7,7 @@ CB = C // P
 TB = T // P
 TG = 2
 GB = TB // TG
-STORE_PIECES = 4
 TEMPERATURE = 0.1
-BANK = 512
-WARM_UP = 3
 
 F32, BF16, U16 = mybir.dt.float32, mybir.dt.bfloat16, mybir.dt.uint16
 FUNC = mybir.ActivationFunctionType
@@ -44,19 +41,12 @@ def tile_entityclusteringhead_kernel(tc, base, tokens, centroids, offs, out):
         for cb in range(CB):
             queue[cb].dma_start(window[cb][:], base[block(cb), :])
 
-        zeros = held.tile([P, BANK], BF16, name="zeros")
-        nc.vector.memset(zeros[:], 0.0)
         ones = held.tile([P, P], BF16, name="ones")
         nc.gpsimd.memset(ones[:], 1.0)
         identity = held.tile([P, P], F32, name="identity")
         make_identity(nc, identity[:])
         minus_half = held.tile([P, 1], F32, name="minus_half")
         nc.gpsimd.memset(minus_half[:], -0.5)
-
-        with tc.psum_pool(name="warm_bank", bufs=1) as warm_bank:
-            warm = warm_bank.tile([P, BANK], F32, name="warm")
-            for i in range(WARM_UP):
-                nc.tensor.matmul(warm[:], zeros[:, 0:P], zeros[:], start=True, stop=True)
 
         cen_unit = [held.tile([P, N], BF16, name=f"cen_unit{cb}") for cb in range(CB)]
         tok_bf = [[held.tile([P, GB * P], BF16, name=f"tok_bf{cb}_{g}") for g in range(TG)] for cb in range(CB)]
@@ -124,7 +114,7 @@ def tile_entityclusteringhead_kernel(tc, base, tokens, centroids, offs, out):
                 nc.vector.reciprocal(inv_exp_sum[:, tb : tb + 1], exp_sum[:, tb : tb + 1])
                 a = ring.tile([P, N], BF16, name="a")
                 nc.vector.tensor_scalar_mul(a[:], exp_sim[:], inv_exp_sum[:, tb : tb + 1])
-                nc.tensor.matmul(w[:], ones[:], a[:], start=(tb == 0), stop=(tb == TB - 1))
+                nc.tensor.matmul(w[:], ones[:, 0:P], a[:], start=(tb == 0), stop=(tb == TB - 1))
                 for cb in range(CB):
                     nc.tensor.matmul(
                         pooled[cb][:], tokT_bf[tb][:, block(cb)], a[:], start=(tb == 0), stop=(tb == TB - 1)
@@ -138,6 +128,4 @@ def tile_entityclusteringhead_kernel(tc, base, tokens, centroids, offs, out):
 
         for cb in range(CB):
             nc.vector.tensor_tensor(window[cb][:].indirect(offsets[:]), pooled_sb[cb][:], inv_w[:], MULT)
-            for piece in range(STORE_PIECES):
-                columns = slice(piece * S // STORE_PIECES, (piece + 1) * S // STORE_PIECES)
-                queue[piece % 2].dma_start(out[block(cb), columns], window[cb][:, columns])
+            queue[cb].dma_start(out[block(cb), :], window[cb][:])

@@ -86,7 +86,7 @@ def tile_entityclusteringhead_kernel(tc, base, tokens, centroids, offs, out):
             prepare_tokens(0)
 
             spread = cen_banks.tile([P, N], F32, name="spread")
-            nc.tensor.matmul(spread[:], inv_nc[:, 0:1].to_broadcast([P, P]), identity[:], start=True, stop=True)
+            nc.tensor.transpose(spread[:], inv_nc[:, 0:1].to_broadcast([P, P]), identity[:])
             for cb in range(CB):
                 nc.vector.tensor_tensor(cen_unit[cb][:], cen[cb][:], spread[:], MULT)
 

@@ -41,12 +41,12 @@ def tile_entityclusteringhead_kernel(tc, base, tokens, centroids, offs, out):
         for cb in range(CB):
             queue[cb].dma_start(window[cb][:], base[block(cb), :])
 
-        ones = held.tile([P, P], BF16, name="ones")
-        nc.gpsimd.memset(ones[:], 1.0)
         identity = held.tile([P, P], F32, name="identity")
         make_identity(nc, identity[:])
+        ones = held.tile([P, P], BF16, name="ones")
+        nc.vector.memset(ones[:], 1.0)
         minus_half = held.tile([P, 1], F32, name="minus_half")
-        nc.gpsimd.memset(minus_half[:], -0.5)
+        nc.vector.memset(minus_half[:], -0.5)
 
         cen_unit = [held.tile([P, N], BF16, name=f"cen_unit{cb}") for cb in range(CB)]
         tok_bf = [[held.tile([P, GB * P], BF16, name=f"tok_bf{cb}_{g}") for g in range(TG)] for cb in range(CB)]

@@ -24,7 +24,7 @@ def tile_entityclusteringhead_kernel(tc, base, tokens, centroids, offs, out):
     nc = tc.nc
     with (
         tc.tile_pool(name="held", bufs=1) as held,
-        tc.tile_pool(name="ring", bufs=2) as ring,
+        tc.tile_pool(name="ring", bufs=TB) as ring,
         tc.psum_pool(name="sim_banks", bufs=2) as sim_banks,
     ):
         queue = [nc.sync, nc.scalar]

@@ -25,7 +25,7 @@ def tile_entityclusteringhead_kernel(tc, base, tokens, centroids, offs, out):
     with (
         tc.tile_pool(name="held", bufs=1) as held,
         tc.tile_pool(name="ring", bufs=TB) as ring,
-        tc.psum_pool(name="sim_banks", bufs=2) as sim_banks,
+        tc.psum_pool(name="sim_banks", bufs=TB) as sim_banks,
     ):
         queue = [nc.sync, nc.scalar]
         cen = [held.tile([P, N], F32, name=f"cen{cb}") for cb in range(CB)]
@@ -53,10 +53,7 @@ def tile_entityclusteringhead_kernel(tc, base, tokens, centroids, offs, out):
         tokT_bf = [held.tile([P, C], BF16, name=f"tokT_bf{tb}") for tb in range(TB)]
         nt2 = held.tile([P, TB], F32, name="nt2")
         sharp = held.tile([P, TB], F32, name="sharp")
-        with (
-            tc.psum_pool(name="cen_banks", bufs=1) as cen_banks,
-            tc.psum_pool(name="flip_banks", bufs=TB) as flip_banks,
-        ):
+        with tc.psum_pool(name="flip_banks", bufs=TB) as flip_banks:
 
             def prepare_tokens(g):
                 for cb in range(CB):
@@ -73,7 +70,7 @@ def tile_entityclusteringhead_kernel(tc, base, tokens, centroids, offs, out):
                     nc.gpsimd.tensor_tensor(sharp[:, tb : tb + 1], nt2[:, tb : tb + 1], minus_half[:], POW)
                     nc.vector.tensor_copy(tokT_bf[tb][:], flipped[:])
 
-            nc2 = cen_banks.tile([P, 1], F32, name="nc2")
+            nc2 = sim_banks.tile([P, 1], F32, name="nc2", tag="sim")
             for cb in range(CB):
                 cen_sq = held.tile([P, N], BF16, name=f"cen_sq{cb}")
                 nc.vector.tensor_tensor(cen_sq[:], cen[cb][:], cen[cb][:], MULT)
@@ -85,7 +82,7 @@ def tile_entityclusteringhead_kernel(tc, base, tokens, centroids, offs, out):
 
             prepare_tokens(0)
 
-            spread = cen_banks.tile([P, N], F32, name="spread")
+            spread = sim_banks.tile([P, N], F32, name="spread", tag="sim")
             nc.tensor.transpose(spread[:], inv_nc[:, 0:1].to_broadcast([P, P]), identity[:])
             for cb in range(CB):
                 nc.vector.tensor_tensor(cen_unit[cb][:], cen[cb][:], spread[:], MULT)

@@ -80,14 +80,13 @@ def tile_entityclusteringhead_kernel(tc, base, tokens, centroids, offs, out):
             inv_nc = held.tile([P, 1], F32, name="inv_nc")
             nc.gpsimd.tensor_tensor(inv_nc[:], nc2_sb[:], minus_half[:], POW)
 
-            prepare_tokens(0)
+            for g in range(TG):
+                prepare_tokens(g)
 
             spread = sim_banks.tile([P, N], F32, name="spread", tag="sim")
             nc.tensor.transpose(spread[:], inv_nc[:, 0:1].to_broadcast([P, P]), identity[:])
             for cb in range(CB):
                 nc.vector.tensor_tensor(cen_unit[cb][:], cen[cb][:], spread[:], MULT)
-
-            prepare_tokens(1)
 
         with tc.psum_pool(name="sum_banks", bufs=1) as sum_banks:
             exp_sum = held.tile([P, TB], F32, name="exp_sum")

@@ -45,7 +45,7 @@ def tile_entityclusteringhead_kernel(tc, base, tokens, centroids, offs, out):
         make_identity(nc, identity[:])
         ones = held.tile([P, P], BF16, name="ones")
         nc.vector.memset(ones[:], 1.0)
-        minus_half = held.tile([P, 1], F32, name="minus_half")
+        minus_half = held.tile([P, GB], F32, name="minus_half")
         nc.vector.memset(minus_half[:], -0.5)
 
         cen_unit = [held.tile([P, N], BF16, name=f"cen_unit{cb}") for cb in range(CB)]
@@ -67,8 +67,10 @@ def tile_entityclusteringhead_kernel(tc, base, tokens, centroids, offs, out):
                     nc.scalar.activation(
                         squares[:], flipped[:], FUNC.Square, scale=TEMPERATURE, accum_out=nt2[:, tb : tb + 1]
                     )
-                    nc.gpsimd.tensor_tensor(sharp[:, tb : tb + 1], nt2[:, tb : tb + 1], minus_half[:], POW)
                     nc.vector.tensor_copy(tokT_bf[tb][:], flipped[:])
+                nc.gpsimd.tensor_tensor(
+                    sharp[:, g * GB : (g + 1) * GB], nt2[:, g * GB : (g + 1) * GB], minus_half[:], POW
+                )
 
             nc2 = sim_banks.tile([P, 1], F32, name="nc2", tag="sim")
             for cb in range(CB):
@@ -78,7 +80,7 @@ def tile_entityclusteringhead_kernel(tc, base, tokens, centroids, offs, out):
             nc2_sb = held.tile([P, 1], F32, name="nc2_sb")
             nc.vector.tensor_copy(nc2_sb[:], nc2[:])
             inv_nc = held.tile([P, 1], F32, name="inv_nc")
-            nc.gpsimd.tensor_tensor(inv_nc[:], nc2_sb[:], minus_half[:], POW)
+            nc.gpsimd.tensor_tensor(inv_nc[:], nc2_sb[:], minus_half[:, 0:1], POW)
 
             for g in range(TG):
                 prepare_tokens(g)

@@ -93,7 +93,7 @@ def tile_entityclusteringhead_kernel(tc, base, tokens, centroids, offs, out):
         with tc.psum_pool(name="sum_banks", bufs=1) as sum_banks:
             exp_sum = held.tile([P, TB], F32, name="exp_sum")
             inv_exp_sum = held.tile([P, TB], F32, name="inv_exp_sum")
-            w = sum_banks.tile([P, N], F32, name="w")
+            w = sum_banks.tile([P, 1], F32, name="w")
             pooled = [sum_banks.tile([P, N], F32, name=f"pooled{cb}") for cb in range(CB)]
             for tb in range(TB):
                 sim = sim_banks.tile([P, N], F32, name="sim")
@@ -112,14 +112,18 @@ def tile_entityclusteringhead_kernel(tc, base, tokens, centroids, offs, out):
                 nc.vector.reciprocal(inv_exp_sum[:, tb : tb + 1], exp_sum[:, tb : tb + 1])
                 a = ring.tile([P, N], BF16, name="a")
                 nc.vector.tensor_scalar_mul(a[:], exp_sim[:], inv_exp_sum[:, tb : tb + 1])
-                nc.tensor.matmul(w[:], ones[:, 0:P], a[:], start=(tb == 0), stop=(tb == TB - 1))
+                nc.tensor.matmul(w[:], a[:], ones[:, 0:1], start=(tb == 0), stop=(tb == TB - 1))
                 for cb in range(CB):
                     nc.tensor.matmul(
                         pooled[cb][:], tokT_bf[tb][:, block(cb)], a[:], start=(tb == 0), stop=(tb == TB - 1)
                     )
 
+            inv_w_column = held.tile([P, 1], F32, name="inv_w_column")
+            nc.vector.reciprocal(inv_w_column[:], w[:])
+            inv_w_ps = sum_banks.tile([P, N], F32, name="inv_w_ps")
+            nc.tensor.transpose(inv_w_ps[:], inv_w_column[:, 0:1].to_broadcast([P, P]), identity[:])
             inv_w = held.tile([P, N], F32, name="inv_w")
-            nc.vector.reciprocal(inv_w[:], w[:])
+            nc.vector.tensor_copy(inv_w[:], inv_w_ps[:])
             pooled_sb = [held.tile([P, N], F32, name=f"pooled_sb{cb}") for cb in range(CB)]
             for cb in range(CB):
                 nc.scalar.copy(pooled_sb[cb][:], pooled[cb][:])

@@ -122,11 +122,11 @@ def tile_entityclusteringhead_kernel(tc, base, tokens, centroids, offs, out):
             nc.vector.reciprocal(inv_w_column[:], w[:])
             inv_w_ps = sum_banks.tile([P, N], F32, name="inv_w_ps")
             nc.tensor.transpose(inv_w_ps[:], inv_w_column[:, 0:1].to_broadcast([P, P]), identity[:])
-            inv_w = held.tile([P, N], F32, name="inv_w")
-            nc.vector.tensor_copy(inv_w[:], inv_w_ps[:])
             pooled_sb = [held.tile([P, N], F32, name=f"pooled_sb{cb}") for cb in range(CB)]
             for cb in range(CB):
-                nc.scalar.copy(pooled_sb[cb][:], pooled[cb][:])
+                nc.vector.tensor_copy(pooled_sb[cb][:], pooled[cb][:])
+            inv_w = held.tile([P, N], F32, name="inv_w")
+            nc.vector.tensor_copy(inv_w[:], inv_w_ps[:])
 
         for cb in range(CB):
             nc.vector.tensor_tensor(window[cb][:].indirect(offsets[:]), pooled_sb[cb][:], inv_w[:], MULT)

@@ -27,19 +27,18 @@ def tile_entityclusteringhead_kernel(tc, base, tokens, centroids, offs, out):
         tc.tile_pool(name="ring", bufs=TB) as ring,
         tc.psum_pool(name="sim_banks", bufs=TB) as sim_banks,
     ):
-        queue = [nc.sync, nc.scalar]
         cen = [held.tile([P, N], F32, name=f"cen{cb}") for cb in range(CB)]
         tok = [[held.tile([P, GB * P], F32, name=f"tok{cb}_{g}") for g in range(TG)] for cb in range(CB)]
         offsets = held.tile([P, N // 16], U16, name="offsets")
         window = [held.tile([P, S], F32, name=f"window{cb}") for cb in range(CB)]
         for cb in range(CB):
-            queue[cb].dma_start(cen[cb][:], centroids[block(cb), :])
+            nc.sync.dma_start(cen[cb][:], centroids[block(cb), :])
         for g in range(TG):
             for cb in range(CB):
-                queue[cb].dma_start(tok[cb][g][:], tokens[block(cb), g * GB * P : (g + 1) * GB * P])
+                nc.sync.dma_start(tok[cb][g][:], tokens[block(cb), g * GB * P : (g + 1) * GB * P])
         nc.sync.dma_start(offsets[:], offs)
         for cb in range(CB):
-            queue[cb].dma_start(window[cb][:], base[block(cb), :])
+            nc.sync.dma_start(window[cb][:], base[block(cb), :])
 
         identity = held.tile([P, P], F32, name="identity")
         make_identity(nc, identity[:])
@@ -130,4 +129,4 @@ def tile_entityclusteringhead_kernel(tc, base, tokens, centroids, offs, out):
 
         for cb in range(CB):
             nc.vector.tensor_tensor(window[cb][:].indirect(offsets[:]), pooled_sb[cb][:], inv_w[:], MULT)
-            queue[cb].dma_start(out[block(cb), :], window[cb][:])
+            nc.sync.dma_start(out[block(cb), :], window[cb][:])

@@ -11,7 +11,7 @@ TEMPERATURE = 0.1
 
 F32, BF16, U16 = mybir.dt.float32, mybir.dt.bfloat16, mybir.dt.uint16
 FUNC = mybir.ActivationFunctionType
-MULT, POW = mybir.AluOpType.mult, mybir.AluOpType.pow
+MULT, ADD, POW = mybir.AluOpType.mult, mybir.AluOpType.add, mybir.AluOpType.pow
 
 FLOPS = 2 * T * N * C + 2 * C * N * T
 
@@ -52,11 +52,14 @@ def tile_entityclusteringhead_kernel(tc, base, tokens, centroids, offs, out):
         tokT_bf = [held.tile([P, C], BF16, name=f"tokT_bf{tb}") for tb in range(TB)]
         nt2 = held.tile([P, TB], F32, name="nt2")
         sharp = held.tile([P, TB], F32, name="sharp")
+        row_sums = held.tile([P, CB * TG], F32, name="row_sums")
         with tc.psum_pool(name="flip_banks", bufs=TB) as flip_banks:
 
             def prepare_tokens(g):
                 for cb in range(CB):
-                    nc.vector.tensor_copy(tok_bf[cb][g][:], tok[cb][g][:])
+                    nc.vector.tensor_scalar(
+                        tok_bf[cb][g][:], tok[cb][g][:], 1.0, None, MULT, ADD, accum_out=row_sums[:, CB * g + cb : CB * g + cb + 1]
+                    )
                 for b in range(GB):
                     tb = g * GB + b
                     flipped = flip_banks.tile([P, C], F32, name="flipped")

import concourse.mybir as mybir
from concourse.masks import make_identity

P = 128
C, T, S, N = 256, 512, 1024, 128
CB = C // P
TB = T // P
TG = 2
GB = TB // TG
TEMPERATURE = 0.1

F32, BF16, U16 = mybir.dt.float32, mybir.dt.bfloat16, mybir.dt.uint16
FUNC = mybir.ActivationFunctionType
MULT, ADD, POW = mybir.AluOpType.mult, mybir.AluOpType.add, mybir.AluOpType.pow

FLOPS = 2 * T * N * C + 2 * C * N * T


def block(i):
    return slice(i * P, (i + 1) * P)


def tile_entityclusteringhead_kernel(tc, base, tokens, centroids, offs, out):
    nc = tc.nc
    with (
        tc.tile_pool(name="held", bufs=1) as held,
        tc.tile_pool(name="ring", bufs=TB) as ring,
        tc.psum_pool(name="sim_banks", bufs=TB) as sim_banks,
    ):
        cen = [held.tile([P, N], F32, name=f"cen{cb}") for cb in range(CB)]
        tok = [[held.tile([P, GB * P], F32, name=f"tok{cb}_{g}") for g in range(TG)] for cb in range(CB)]
        offsets = held.tile([P, N // 16], U16, name="offsets")
        window = [held.tile([P, S], F32, name=f"window{cb}") for cb in range(CB)]
        for cb in range(CB):
            nc.sync.dma_start(cen[cb][:], centroids[block(cb), :])
        for g in range(TG):
            for cb in range(CB):
                nc.sync.dma_start(tok[cb][g][:], tokens[block(cb), g * GB * P : (g + 1) * GB * P])
        nc.sync.dma_start(offsets[:], offs)
        for cb in range(CB):
            nc.sync.dma_start(window[cb][:], base[block(cb), :])

        identity = held.tile([P, P], F32, name="identity")
        make_identity(nc, identity[:])
        ones = held.tile([P, P], BF16, name="ones")
        nc.vector.memset(ones[:], 1.0)
        minus_half = held.tile([P, GB], F32, name="minus_half")
        nc.vector.memset(minus_half[:], -0.5)

        cen_unit = [held.tile([P, N], BF16, name=f"cen_unit{cb}") for cb in range(CB)]
        tok_bf = [[held.tile([P, GB * P], BF16, name=f"tok_bf{cb}_{g}") for g in range(TG)] for cb in range(CB)]
        tokT_bf = [held.tile([P, C], BF16, name=f"tokT_bf{tb}") for tb in range(TB)]
        nt2 = held.tile([P, TB], F32, name="nt2")
        sharp = held.tile([P, TB], F32, name="sharp")
        row_sums = held.tile([P, CB * TG], F32, name="row_sums")
        with tc.psum_pool(name="flip_banks", bufs=TB) as flip_banks:

            def prepare_tokens(g):
                for cb in range(CB):
                    nc.vector.tensor_scalar(
                        tok_bf[cb][g][:], tok[cb][g][:], 1.0, None, MULT, ADD, accum_out=row_sums[:, CB * g + cb : CB * g + cb + 1]
                    )
                for b in range(GB):
                    tb = g * GB + b
                    flipped = flip_banks.tile([P, C], F32, name="flipped")
                    for cb in range(CB):
                        nc.tensor.transpose(flipped[:, block(cb)], tok[cb][g][:, block(b)], identity[:])
                    squares = ring.tile([P, C], BF16, name="squares")
                    nc.scalar.activation(
                        squares[:], flipped[:], FUNC.Square, scale=TEMPERATURE, accum_out=nt2[:, tb : tb + 1]
                    )
                    nc.vector.tensor_copy(tokT_bf[tb][:], flipped[:])
                nc.gpsimd.tensor_tensor(
                    sharp[:, g * GB : (g + 1) * GB], nt2[:, g * GB : (g + 1) * GB], minus_half[:], POW
                )

            nc2 = sim_banks.tile([P, 1], F32, name="nc2", tag="sim")
            for cb in range(CB):
                cen_sq = held.tile([P, N], BF16, name=f"cen_sq{cb}")
                nc.vector.tensor_tensor(cen_sq[:], cen[cb][:], cen[cb][:], MULT)
                nc.tensor.matmul(nc2[:], cen_sq[:], ones[:, 0:1], start=(cb == 0), stop=(cb == CB - 1))
            nc2_sb = held.tile([P, 1], F32, name="nc2_sb")
            nc.vector.tensor_copy(nc2_sb[:], nc2[:])
            inv_nc = held.tile([P, 1], F32, name="inv_nc")
            nc.gpsimd.tensor_tensor(inv_nc[:], nc2_sb[:], minus_half[:, 0:1], POW)

            for g in range(TG):
                prepare_tokens(g)

            spread = sim_banks.tile([P, N], F32, name="spread", tag="sim")
            nc.tensor.transpose(spread[:], inv_nc[:, 0:1].to_broadcast([P, P]), identity[:])
            for cb in range(CB):
                nc.vector.tensor_tensor(cen_unit[cb][:], cen[cb][:], spread[:], MULT)

        with tc.psum_pool(name="sum_banks", bufs=1) as sum_banks:
            exp_sum = held.tile([P, TB], F32, name="exp_sum")
            inv_exp_sum = held.tile([P, TB], F32, name="inv_exp_sum")
            w = sum_banks.tile([P, 1], F32, name="w")
            pooled = [sum_banks.tile([P, N], F32, name=f"pooled{cb}") for cb in range(CB)]
            for tb in range(TB):
                sim = sim_banks.tile([P, N], F32, name="sim")
                for cb in range(CB):
                    nc.tensor.matmul(
                        sim[:],
                        tok_bf[cb][tb // GB][:, block(tb % GB)],
                        cen_unit[cb][:],
                        start=(cb == 0),
                        stop=(cb == CB - 1),
                    )
                exp_sim = ring.tile([P, N], F32, name="exp_sim")
                nc.scalar.activation(
                    exp_sim[:], sim[:], FUNC.Exp, scale=sharp[:, tb : tb + 1], accum_out=exp_sum[:, tb : tb + 1]
                )
                nc.vector.reciprocal(inv_exp_sum[:, tb : tb + 1], exp_sum[:, tb : tb + 1])
                a = ring.tile([P, N], BF16, name="a")
                nc.vector.tensor_scalar_mul(a[:], exp_sim[:], inv_exp_sum[:, tb : tb + 1])
                nc.tensor.matmul(w[:], a[:], ones[:, 0:1], start=(tb == 0), stop=(tb == TB - 1))
                for cb in range(CB):
                    nc.tensor.matmul(
                        pooled[cb][:], tokT_bf[tb][:, block(cb)], a[:], start=(tb == 0), stop=(tb == TB - 1)
                    )

            inv_w_column = held.tile([P, 1], F32, name="inv_w_column")
            nc.vector.reciprocal(inv_w_column[:], w[:])
            inv_w_ps = sum_banks.tile([P, N], F32, name="inv_w_ps")
            nc.tensor.transpose(inv_w_ps[:], inv_w_column[:, 0:1].to_broadcast([P, P]), identity[:])
            pooled_sb = [held.tile([P, N], F32, name=f"pooled_sb{cb}") for cb in range(CB)]
            for cb in range(CB):
                nc.vector.tensor_copy(pooled_sb[cb][:], pooled[cb][:])
            inv_w = held.tile([P, N], F32, name="inv_w")
            nc.vector.tensor_copy(inv_w[:], inv_w_ps[:])

        for cb in range(CB):
            nc.vector.tensor_tensor(window[cb][:].indirect(offsets[:]), pooled_sb[cb][:], inv_w[:], MULT)
            nc.sync.dma_start(out[block(cb), :], window[cb][:])
